import numpy as np
import ml_dtypes


def mxq(x, axis, fmt="e4m3"):
    dtype, down = {"e4m3": (ml_dtypes.float8_e4m3fn, 7), "e5m2": (ml_dtypes.float8_e5m2, 14)}[fmt]
    v = np.moveaxis(np.asarray(x, np.float32).astype(ml_dtypes.bfloat16).astype(np.float64), axis, -1)
    blocks = v.reshape(v.shape[:-1] + (-1, 32))
    amax = np.abs(blocks).max(-1, keepdims=True)
    byte = np.maximum(np.where(amax > 0, np.frexp(amax)[1] - 1 + 127, 0) - down, 1)
    scale = np.exp2(byte - 127.0)
    codes = (blocks / scale).astype(np.float32).astype(dtype).astype(np.float64)
    return np.moveaxis((codes * scale).reshape(v.shape), -1, axis)


WIDE = False


def mx_kscale(k):
    if not WIDE:
        return np.ones(k)
    levels = np.array([18, -18])
    if k % 512:
        return np.exp2(np.random.permutation(np.resize(levels, k // 32))).repeat(32)
    a = np.empty((k // 512, 16))
    for p in range(k // 512):
        a[p, :8] = np.random.permutation(np.resize(levels, 8))
        for g in range(8):
            far = levels[np.abs(levels - a[p, g]) >= 10]
            a[p, g + 8] = far[np.random.randint(len(far))]
    return np.exp2(a.ravel()).repeat(32)


BF16 = ml_dtypes.bfloat16


def bf(x):
    return np.asarray(x, np.float32).astype(BF16)


def f64(x):
    return np.asarray(x).astype(np.float64)


B, HD, XO = 1024, 1536, 1024


def setup_inputs():
    n = np.random.standard_normal
    s = mx_kscale(B)[:, None]
    u = mx_kscale(XO)
    hd0 = bf(np.tanh(n((B, HD))))
    wm0 = bf(n((XO, HD)) * 1.5 / np.sqrt(HD))
    b_mu_d = bf(n(XO) * 0.3)
    wl0 = bf(n((XO, HD)) * 1.5 / np.sqrt(HD))
    b_ls_d = bf(n(XO) * 0.3)
    eps_x = bf(n((B, XO)))
    g = bf(n((B, XO)) * np.exp2(np.random.randint(-6, 1, (B, 1))) * 4.0 / s * u)
    ls = f64(hd0) @ f64(wl0).T + f64(b_ls_d)
    return {"hd": bf(f64(hd0) * s),
            "W_mu_d": bf(f64(wm0) / u[:, None]),
            "b_mu_d": b_mu_d,
            "W_ls_d": bf(f64(wl0) / u[:, None]),
            "b_ls_d": b_ls_d,
            "eps_x": eps_x,
            "ls": np.asarray(ls, np.float32),
            "grad_out": g}


def reference(hd, W_mu_d, b_mu_d, W_ls_d, b_ls_d, eps_x, ls, grad_out):
    g = f64(grad_out)
    dls = g * (0.5 * np.exp(0.5 * f64(ls)) * f64(eps_x))
    dhd = ((mxq(g, 1, "e5m2") @ mxq(f64(W_mu_d), 0, "e4m3"))
           + (mxq(dls, 1, "e5m2") @ mxq(f64(W_ls_d), 0, "e4m3")))
    dw = mxq(dls, 0, "e5m2").T @ mxq(f64(hd), 0, "e4m3")
    return dhd, dw

from contextlib import ExitStack

import concourse.mybir as mybir
from concourse.masks import make_identity

TOKENS, HIDDEN, FEATURES = 1024, 1536, 1024
FLOPS = 3 * 2 * TOKENS * HIDDEN * FEATURES

F32 = mybir.dt.float32
BF16 = mybir.dt.bfloat16
U32 = mybir.dt.uint32
U8 = mybir.dt.uint8
E4M3 = mybir.dt.float8_e4m3fn_x4
E5M2 = mybir.dt.float8_e5m2_x4
MULT = mybir.AluOpType.mult
EXP = mybir.ActivationFunctionType.Exp

P = 128
PACK = 4
K = P * PACK
N = 512
PASSES = 2
THIRDS = HIDDEN // N

CHUNKS = 4
ROWS = 2


def tile_vae_pb_v_kernel(tc, hd, W_mu_d, b_mu_d, W_ls_d, b_ls_d, eps_x, ls, grad_out, out_0, out_1):
    nc = tc.nc
    on_vector = nc.vector.tensor_copy
    on_scalar = nc.scalar.copy

    rows_of_four = "(g p j) w -> g p j w"
    logvar_in = ls.rearrange(rows_of_four, p=P, j=PACK)
    eps_in = eps_x.rearrange(rows_of_four, p=P, j=PACK)
    grad_in = grad_out.rearrange(rows_of_four, p=P, j=PACK)
    out_0_rows = out_0.rearrange(rows_of_four, p=P, j=PACK)
    weight_in = {
        "mu": W_mu_d.rearrange(rows_of_four, p=P, j=PACK),
        "ls": W_ls_d.rearrange(rows_of_four, p=P, j=PACK),
        "hd": hd.rearrange(rows_of_four, p=P, j=PACK),
    }

    with ExitStack() as ctx:
        keep = ctx.enter_context(tc.tile_pool(name="keep", bufs=1))
        work = ctx.enter_context(tc.tile_pool(name="work", bufs=1))
        psum = ctx.enter_context(tc.psum_pool(name="psum", bufs=1))
        ctx.enter_context(tc.manual_schedule())

        identity = keep.tile([P, P], F32, name="identity")
        make_identity(nc, identity[:])

        dls = [keep.tile([P, PACK, FEATURES], BF16, name="dls%d" % g, align_bytes=64) for g in range(PASSES)]

        grad, logvar, product = {}, {}, {}
        weight, weight_codes, weight_scales = {}, {}, {}
        token_codes, token_scales = {}, {}
        feature_codes, feature_scales = {}, {}
        side_by_side, transposed, sums, result = {}, {}, {}, {}

        def load_grad(c, first=0, count=ROWS):
            if c not in grad:
                grad[c] = work.tile([P, ROWS, FEATURES], BF16, name="grad", bufs=CHUNKS, align_bytes=64)
            j = ROWS * (c % 2) + first
            nc.sync.dma_start(out=grad[c][:, first : first + count, :], in_=grad_in[c // 2][:, j : j + count, :])

        def load_eps(c, first=0, count=ROWS):
            j = ROWS * (c % 2) + first
            nc.sync.dma_start(out=dls[c // 2][:, j : j + count, :], in_=eps_in[c // 2][:, j : j + count, :])

        def load_logvar(c, first=0, count=ROWS):
            if c not in logvar:
                logvar[c] = work.tile([P, ROWS, FEATURES], F32, name="logvar", bufs=3, align_bytes=64)
            j = ROWS * (c % 2) + first
            nc.sync.dma_start(out=logvar[c][:, first : first + count, :], in_=logvar_in[c // 2][:, j : j + count, :])

        def load_weight(name, g):
            weight[name, g] = work.tile([P, PACK, HIDDEN], BF16, name="weight", bufs=4, align_bytes=64)
            nc.sync.dma_start(out=weight[name, g][:], in_=weight_in[name][g])
            weight_codes[name, g] = keep.tile([P, HIDDEN], U32, name="codes_%s%d" % (name, g), align_bytes=64)
            weight_scales[name, g] = keep.tile([P, HIDDEN], U8, name="scales_%s%d" % (name, g), align_bytes=64)

        def new_side_by_side(shape):
            return work.tile(shape, BF16, name="side_by_side", bufs=6, align_bytes=64)

        def join_rows(tile, source, copy):
            copy(
                out=tile[:].rearrange("p (c i) j -> p c j i", i=4),
                in_=source.rearrange("p j (c i) -> p c j i", i=4),
            )

        def join_weight(name, g, h, copy):
            tile = side_by_side[name, g, h] = new_side_by_side([P, N, PACK])
            join_rows(tile, weight[name, g][:, :, h * N : (h + 1) * N], copy)

        def quantize_weight(name, g, h):
            cols = slice(h * N, (h + 1) * N)
            nc.vector.quantize_mx(
                out=weight_codes[name, g][:, cols].bitcast(E4M3),
                scales=weight_scales[name, g][:, cols],
                in_=side_by_side[name, g, h][:].rearrange("p c j -> p (c j)"),
            )

        def join_tokens(g, x, copy):
            tile = side_by_side["tokens", g, x] = new_side_by_side([P, N, PACK])
            join_rows(tile, dls[g][:, :, x * N : (x + 1) * N], copy)

        def quantize_tokens(g, x):
            token_codes[g, x] = keep.tile([P, N], U32, name="token_codes%d%d" % (g, x), align_bytes=64)
            token_scales[g, x] = keep.tile([P, N], U8, name="token_scales%d%d" % (g, x), align_bytes=64)
            nc.vector.quantize_mx(
                out=token_codes[g, x][:].bitcast(E5M2),
                scales=token_scales[g, x][:],
                in_=side_by_side["tokens", g, x][:].rearrange("p c j -> p (c j)"),
            )

        def dls_row(c, i):
            return dls[c // 2][:, ROWS * (c % 2) + i, :]

        def times_eps(c, i):
            if c not in product:
                product[c] = work.tile([P, ROWS, FEATURES], F32, name="product", align_bytes=64)
            nc.vector.scalar_tensor_tensor(
                out=product[c][:, i, :], in0=grad[c][:, i, :], scalar=0.5, in1=dls_row(c, i), op0=MULT, op1=MULT
            )

        def exponential(c, i):
            nc.scalar.activation(out=logvar[c][:, i, :], in_=logvar[c][:, i, :], func=EXP, scale=0.5)

        def times_exponential(c, i):
            nc.vector.tensor_tensor(out=dls_row(c, i), in0=product[c][:, i, :], in1=logvar[c][:, i, :], op=MULT)

        def transpose(kind, c):
            for i in range(ROWS):
                tile = transposed[kind, c, i] = psum.tile([P, PASSES, 2, P], F32, name="transposed", bufs=2)
                words = (grad[c][:, i, :] if kind == "grad" else dls_row(c, i)).bitcast(F32)
                for x in range(PASSES):
                    for odd in range(2):
                        picked = words[:, x * K // 2 + odd : (x + 1) * K // 2 : 2]
                        nc.tensor.transpose(tile[:, x, odd, :], picked, identity[:])

        def join_words(kind, c, i, copy):
            if (kind, c) not in side_by_side:
                side_by_side[kind, c] = new_side_by_side([P, ROWS, PASSES, P, PACK])
            copy(
                out=side_by_side[kind, c][:, i].bitcast(F32),
                in_=transposed[kind, c, i][:].rearrange("p x odd r -> p x r odd"),
            )

        def quantize_features(kind, c):
            width = ROWS * PASSES * P
            feature_codes[kind, c] = keep.tile([P, width], U32, name="%s_codes%d" % (kind, c), align_bytes=64)
            feature_scales[kind, c] = keep.tile([P, width], U8, name="%s_scales%d" % (kind, c), align_bytes=64)
            nc.vector.quantize_mx(
                out=feature_codes[kind, c][:].bitcast(E5M2),
                scales=feature_scales[kind, c][:],
                in_=side_by_side[kind, c][:].rearrange("p i x r k -> p (i x r k)"),
            )

        def matmul_pass(out, codes, scales, first, name, g, h, start, stop):
            still = slice(first, first + P)
            cols = slice(h * N, (h + 1) * N)
            nc.tensor.matmul_mx(
                out=out[:],
                lhsT=codes[:, still].bitcast(E5M2),
                lhsT_scale=scales[:, still],
                rhs=weight_codes[name, g][:, cols].bitcast(E4M3),
                rhs_scale=weight_scales[name, g][:, cols],
                start=start,
                stop=stop,
            )

        def new_sum(bank):
            return psum.tile([P, N], F32, name="bank%d" % bank)

        def out_0_mu(c, i, h, x):
            if x == 0:
                sums[c, i, h] = new_sum(THIRDS * i + h)
            first = (PASSES * i + x) * P
            matmul_pass(
                sums[c, i, h], feature_codes["grad", c], feature_scales["grad", c], first, "mu", x, h, x == 0, False
            )

        def out_0_ls(c, i, h, x):
            first = (PASSES * i + x) * P
            matmul_pass(
                sums[c, i, h], feature_codes["dls", c], feature_scales["dls", c], first, "ls", x, h, False, x == 1
            )

        def out_0_copy(c, i, h, copy):
            if (c, i) not in result:
                result[c, i] = work.tile([P, HIDDEN], F32, name="result", bufs=4, align_bytes=64)
            copy(out=result[c, i][:, h * N : (h + 1) * N], in_=sums[c, i, h][:])

        def out_0_store(c, i, cols):
            j = ROWS * (c % 2) + i
            nc.sync.dma_start(out=out_0_rows[c // 2][:, j, cols], in_=result[c, i][:, cols])

        def out_1_group(m, h):
            tile = sums["out_1", m, h] = new_sum((FEATURES // P * h + m) % 6)
            x, first = m // 4, m % 4 * P
            for g in range(PASSES):
                matmul_pass(tile, token_codes[g, x], token_scales[g, x], first, "hd", g, h, g == 0, g == 1)

        def out_1_copy(m, h, copy):
            pair = ("out_1", m // 2, h)
            if pair not in result:
                result[pair] = work.tile([P, 2, N], F32, name="result", bufs=4, align_bytes=64)
            copy(out=result[pair][:, m % 2, :], in_=sums["out_1", m, h][:])

        def out_1_store(m, h, count):
            rows = out_1[m * P : (m + count) * P, h * N : (h + 1) * N].rearrange("(a p) w -> p a w", p=P)
            nc.sync.dma_start(out=rows, in_=result["out_1", m // 2, h][:, m % 2 : m % 2 + count, :])

        both = range(ROWS)
        whole_row = slice(0, HIDDEN)

        def chunk_0(product_pass, x, thirds):
            for h in thirds:
                for i in both:
                    product_pass(0, i, h, x)

        load_weight("mu", 0)
        for i in both:
            load_grad(0, i, 1)
            load_eps(0, i, 1)
        for i in both:
            load_logvar(0, i, 1)
        load_weight("mu", 1)
        load_weight("ls", 0)
        load_grad(1)
        load_weight("ls", 1)
        load_eps(1)
        load_logvar(1)
        load_grad(2)
        load_eps(2)
        load_logvar(2)

        join_weight("mu", 0, 0, on_vector)
        join_weight("mu", 0, 1, on_scalar)
        transpose("grad", 0)
        for i in both:
            join_words("grad", 0, i, on_scalar)
        for i in both:
            exponential(0, i)
        times_eps(0, 0)
        quantize_weight("mu", 0, 1)
        quantize_weight("mu", 0, 0)
        times_eps(0, 1)
        join_weight("mu", 0, 2, on_scalar)
        quantize_features("grad", 0)
        for i in both:
            times_exponential(0, i)
        chunk_0(out_0_mu, 0, (1, 0))

        join_weight("mu", 1, 1, on_vector)
        join_weight("mu", 1, 0, on_vector)
        join_weight("mu", 1, 2, on_scalar)
        transpose("dls", 0)
        join_words("dls", 0, 0, on_vector)
        join_words("dls", 0, 1, on_scalar)
        quantize_weight("mu", 0, 2)
        for h in (2, 0, 1):
            quantize_weight("mu", 1, h)
        quantize_features("dls", 0)
        chunk_0(out_0_mu, 0, (2,))
        chunk_0(out_0_mu, 1, (2, 1, 0))

        join_weight("ls", 0, 1, on_scalar)
        join_weight("ls", 0, 2, on_vector)
        join_weight("ls", 0, 0, on_scalar)
        quantize_weight("ls", 0, 2)
        quantize_weight("ls", 0, 1)
        join_weight("ls", 1, 2, on_scalar)
        join_weight("ls", 1, 0, on_vector)
        join_weight("ls", 1, 1, on_scalar)
        times_eps(1, 0)
        quantize_weight("ls", 0, 0)
        quantize_weight("ls", 1, 0)
        quantize_weight("ls", 1, 2)
        times_eps(1, 1)
        quantize_weight("ls", 1, 1)
        for i in both:
            exponential(1, i)
        chunk_0(out_0_ls, 0, (2, 1))
        transpose("grad", 1)
        chunk_0(out_0_ls, 0, (0,))
        chunk_0(out_0_ls, 1, (0, 2, 1))
        for i in both:
            join_words("grad", 1, i, on_scalar)
        for i in both:
            times_exponential(1, i)
        quantize_features("grad", 1)

        load_eps(3)
        load_grad(3)
        load_weight("hd", 1)
        load_weight("hd", 0)
        load_logvar(3)
        out_0_copy(0, 0, 0, on_scalar)
        out_0_copy(0, 0, 1, on_scalar)
        out_0_copy(0, 0, 2, on_vector)
        out_0_store(0, 0, whole_row)

        out_1_operands = {
            1: [(join_weight, "hd", 0, 0, on_vector), (quantize_tokens, 0, 0),
                (join_tokens, 0, 1, on_scalar), (quantize_weight, "hd", 0, 0)],
            2: [(join_weight, "hd", 1, 0, on_vector), (join_tokens, 1, 0, on_vector),
                (quantize_weight, "hd", 1, 0), (quantize_tokens, 0, 1)],
            3: [(join_tokens, 1, 1, on_scalar), (join_weight, "hd", 0, 1, on_vector), (quantize_tokens, 1, 0)],
        }
        for c in range(1, CHUNKS):
            n = c + 1
            for h in range(THIRDS):
                out_0_copy(c - 1, 1, h, on_scalar)
            out_0_store(c - 1, 1, whole_row)
            transpose("dls", c)
            join_words("dls", c, 0, on_vector)
            join_words("dls", c, 1, on_scalar)
            if n < CHUNKS:
                times_eps(n, 0)
            quantize_features("dls", c)
            if n < CHUNKS:
                times_eps(n, 1)
                for i in both:
                    exponential(n, i)
            if c == 1:
                join_tokens(0, 0, on_vector)
            for i in both:
                for h in range(THIRDS):
                    for x in range(PASSES):
                        out_0_mu(c, i, h, x)
            if n < CHUNKS:
                transpose("grad", n)
                for i in both:
                    times_exponential(n, i)
                for i in both:
                    join_words("grad", n, i, on_scalar)
                quantize_features("grad", n)
            for h in range(THIRDS):
                for x in range(PASSES):
                    out_0_ls(c, 0, h, x)
            for step, *args in out_1_operands[c]:
                step(*args)
            for h in range(THIRDS):
                out_0_copy(c, 0, h, on_scalar)
                if n == CHUNKS:
                    out_0_store(c, 0, slice(h * N, (h + 1) * N))
            if n < CHUNKS:
                out_0_store(c, 0, whole_row)
            for h in range(THIRDS):
                for x in range(PASSES):
                    out_0_ls(c, 1, h, x)
        for h in range(THIRDS):
            out_0_copy(CHUNKS - 1, 1, h, on_scalar)
            out_0_store(CHUNKS - 1, 1, slice(h * N, (h + 1) * N))

        last_operands = {
            0: [(quantize_weight, "hd", 0, 1)],
            1: [(quantize_tokens, 1, 1), (join_weight, "hd", 1, 1, on_vector), (join_weight, "hd", 1, 2, on_vector)],
            2: [(quantize_weight, "hd", 1, 1), (quantize_weight, "hd", 1, 2)],
            3: [(join_weight, "hd", 0, 2, on_vector)],
            4: [(quantize_weight, "hd", 0, 2)],
        }
        pairs = [(m, h) for h in range(THIRDS) for m in range(0, FEATURES // P, 2)]
        for turn, (m, h) in enumerate(pairs):
            out_1_group(m, h)
            out_1_group(m + 1, h)
            for step, *args in last_operands.get(turn, []):
                step(*args)
            out_1_copy(m, h, on_scalar if turn < 3 else on_vector)
            out_1_copy(m + 1, h, on_scalar)
            if turn + 1 < len(pairs):
                out_1_store(m, h, 2)
            else:
                out_1_store(m, h, 1)
                out_1_store(m + 1, h, 1)
